import numpy as np
import ml_dtypes


def mxq(x, axis, fmt="e4m3"):
    dtype, down = {"e4m3": (ml_dtypes.float8_e4m3fn, 7), "e5m2": (ml_dtypes.float8_e5m2, 14)}[fmt]
    v = np.moveaxis(np.asarray(x, np.float32).astype(ml_dtypes.bfloat16).astype(np.float64), axis, -1)
    blocks = v.reshape(v.shape[:-1] + (-1, 32))
    amax = np.abs(blocks).max(-1, keepdims=True)
    byte = np.maximum(np.where(amax > 0, np.frexp(amax)[1] - 1 + 127, 0) - down, 1)
    scale = np.exp2(byte - 127.0)
    codes = (blocks / scale).astype(np.float32).astype(dtype).astype(np.float64)
    return np.moveaxis((codes * scale).reshape(v.shape), -1, axis)


WIDE = False


def mx_kscale(k):
    if not WIDE:
        return np.ones(k)
    levels = np.array([30, -30])
    if k % 512:
        return np.exp2(np.random.permutation(np.resize(levels, k // 32))).repeat(32)
    a = np.empty((k // 512, 16))
    for p in range(k // 512):
        a[p, :8] = np.random.permutation(np.resize(levels, 8))
        for g in range(8):
            far = levels[np.abs(levels - a[p, g]) >= 10]
            a[p, g + 8] = far[np.random.randint(len(far))]
    return np.exp2(a.ravel()).repeat(32)


BF16 = ml_dtypes.bfloat16


def bf(x):
    return np.asarray(x, np.float32).astype(BF16)


def f64(x):
    return np.asarray(x).astype(np.float64)


E2M1 = np.array([0.0, 0.5, 1.0, 1.5, 2.0, 3.0, 4.0, 6.0, -0.0, -0.5, -1.0, -1.5, -2.0, -3.0, -4.0, -6.0])


def pack_weight(w, fmt):
    k, n = w.shape
    w = f64(bf(w)).reshape(k // 32, 32, n)
    amax = np.abs(w).max(1)
    if fmt == "e4m3":
        byte = np.frexp(amax)[1] - 1 + 127 - 7
    else:
        mant, ex = np.frexp(amax / 6.0)
        byte = np.where(mant > 0.5, ex, ex - 1) + 127
    byte = np.clip(np.where(amax > 0, byte, 1), 1, 254)
    scaled = (w * np.exp2(127.0 - byte)[:, None, :]).reshape(k, n).astype(np.float32)
    by_word = np.ascontiguousarray(scaled.reshape(k // 512, 128, 4, n).transpose(0, 1, 3, 2))
    if fmt == "e4m3":
        words = by_word.astype(ml_dtypes.float8_e4m3fn).view(np.uint8)
    else:
        c = by_word.astype(ml_dtypes.float4_e2m1fn).view(np.uint8) & 0xF
        words = c[..., 0::2] | (c[..., 1::2] << 4)
    return np.ascontiguousarray(words), np.ascontiguousarray(byte.astype(np.uint8).reshape(k // 512, 16, n))


def unpack_weight(words, scales, fmt):
    g, p, n, _ = words.shape
    if fmt == "e4m3":
        vals = np.ascontiguousarray(words).view(ml_dtypes.float8_e4m3fn).astype(np.float64)
    else:
        nib = np.empty((g, p, n, 4), np.uint8)
        nib[..., 0::2] = words & 0xF
        nib[..., 1::2] = words >> 4
        vals = E2M1[nib]
    vals = vals * np.repeat(np.exp2(scales.astype(np.float64) - 127.0), 8, axis=1)[..., None]
    return vals.transpose(0, 1, 3, 2).reshape(g * 512, n)

def pack4(w):
    words, scales = pack_weight(w, "e2m1")
    return words.reshape(words.shape[0], 128, -1), scales


def unpack4(words, scales):
    return unpack_weight(words.reshape(words.shape[0], 128, -1, 2), scales, "e2m1")


B, H, N, D, DT, NH = 8, 128, 128, 1024, 512, 8


def softmax(v, axis):
    e = np.exp(v - v.max(axis=axis, keepdims=True))
    return e / e.sum(axis=axis, keepdims=True)


def setup_inputs():
    s = mx_kscale(DT)
    cand_topics = bf(np.random.standard_normal((B, N, DT)) * s)
    Wq = np.random.standard_normal((D, DT)) * 2.0 / np.sqrt(DT) / s[None, :]
    Wq_words, Wq_scales = pack4(np.ascontiguousarray(Wq.T))
    bq = bf(np.random.standard_normal(D) * 0.5)
    return {"cand_topics": cand_topics,
            "Wq_words": Wq_words,
            "Wq_scales": Wq_scales,
            "bq": bq}


def reference(cand_topics, Wq_words, Wq_scales, bq):
    q = (mxq(f64(cand_topics), 2, "e5m2") @ unpack4(Wq_words, Wq_scales)) + f64(bq)
    query_weights = softmax(np.sqrt((q ** 2).sum(axis=-1)), 1)
    return q, query_weights

@@ -1,0 +1,195 @@
+from contextlib import ExitStack
+
+import concourse.mybir as mybir
+from concourse.masks import make_identity
+
+B, N, K, D = 8, 128, 512, 1024
+FLOPS = 2 * B * N * K * D
+
+F32 = mybir.dt.float32
+BF16 = mybir.dt.bfloat16
+I32 = mybir.dt.int32
+U32 = mybir.dt.uint32
+U8 = mybir.dt.uint8
+E5M2X4 = mybir.dt.float8_e5m2_x4
+E2M1X4 = mybir.dt.float4_e2m1fn_x4
+ACT = mybir.ActivationFunctionType
+ALU = mybir.AluOpType
+AX = mybir.AxisListType
+
+P = 128
+HALF = 512
+GROUPS = [(0,), (1,), (2, 3), (4, 5), (6, 7)]
+
+
+def tile_candidateaware_clickednewsattention_pa_kernel(tc, cand_topics, Wq_words, Wq_scales, bq, out_0, out_1):
+    nc = tc.nc
+    with ExitStack() as ctx:
+        keep = ctx.enter_context(tc.tile_pool(name="keep", bufs=1))
+        rot = ctx.enter_context(tc.tile_pool(name="rot", bufs=2))
+        tps = ctx.enter_context(tc.psum_pool(name="tps", bufs=2))
+        accs = ctx.enter_context(tc.psum_pool(name="accs", bufs=6))
+        ctx.enter_context(tc.manual_schedule())
+
+        ident = keep.tile([P, P], F32, name="ident")
+        norms = keep.tile([P, P], F32, name="norms")
+        ones = keep.tile([P, P], BF16, name="ones")
+        half = keep.tile([P, 1], F32, name="half")
+        bias_row = keep.tile([P, D], BF16, name="bias_row")
+        bias_all = [keep.tile([P, HALF], BF16, name="bias_all%d" % h) for h in range(2)]
+        w_codes = keep.tile([P, 2 * D], U8, name="w_codes", align_bytes=64)
+        w_scales = keep.tile([P, D], U8, name="w_scales", align_bytes=64)
+        x_first = keep.tile([P, 1, K], BF16, name="x_first")
+        x_mid = keep.tile([P, 3, K], BF16, name="x_mid")
+        x_last = keep.tile([P, 4, K], BF16, name="x_last")
+        sumsq = keep.tile([P, B + 1], F32, name="sumsq")
+        sum_last = keep.tile([P, 1], F32, name="sum_last")
+        q_sb = [keep.tile([P, D], F32, name="q%d" % b) for b in range(B)]
+        grouped = [keep.tile([P, len(g) * K], BF16, name="grouped%d" % i, align_bytes=64) for i, g in enumerate(GROUPS)]
+        x_codes = [keep.tile([P, len(g) * N], U32, name="x_codes%d" % i, align_bytes=64) for i, g in enumerate(GROUPS)]
+        x_scales = [keep.tile([P, len(g) * N], U8, name="x_scales%d" % i, align_bytes=64) for i, g in enumerate(GROUPS)]
+
+        def x_rows(b):
+            if b == 0:
+                return x_first[:, 0, :]
+            if b < 4:
+                return x_mid[:, b - 1, :]
+            return x_last[:, b - 4, :]
+
+        where = {}
+        for i, g in enumerate(GROUPS):
+            for j, b in enumerate(g):
+                where[b] = (i, j)
+
+        nc.vector.memset(w_scales[:].bitcast(I32), 0)
+        nc.vector.memset(bias_row[:].bitcast(I32), 0)
+        nc.vector.memset(ones[:], 1.0)
+        make_identity(nc, ident[:])
+        nc.gpsimd.memset(norms[:], 0.0)
+
+        nc.sync.dma_start(out=x_first[:, 0, :], in_=cand_topics[0])
+        nc.scalar.dma_start(out=bias_row[0:1, :], in_=bq.rearrange("(o n) -> o n", o=1))
+        for quad in range(4):
+            nc.sync.dma_start(
+                out=w_scales[32 * quad : 32 * quad + 4, :].bitcast(I32),
+                in_=Wq_scales[0, 4 * quad : 4 * quad + 4, :].bitcast(I32),
+            )
+        nc.sync.dma_start(out=x_mid[:], in_=cand_topics[1:4].rearrange("b n k -> n b k"))
+        nc.sync.dma_start(out=w_codes[:].bitcast(I32), in_=Wq_words[0].bitcast(I32))
+        nc.sync.dma_start(out=x_last[:], in_=cand_topics[4:8].rearrange("b n k -> n b k"))
+
+        nc.scalar.activation(out=half[:], in_=ones[:, 0:1], func=ACT.Copy, scale=0.5)
+
+        turned = {}
+        sums = {}
+        bias_ps = {}
+
+        def turn(i):
+            g = GROUPS[i]
+            xt = tps.tile([P, len(g), 2, N], F32, tag="tp", name="xt%d" % i)
+            for j, b in enumerate(g):
+                words = x_rows(b).bitcast(F32)
+                for u in range(2):
+                    nc.tensor.transpose(xt[:, j, u, :], words[:, u : K // 2 : 2], ident[:])
+            turned[i] = xt
+
+        def interleave(i):
+            nb = len(GROUPS[i])
+            nc.scalar.copy(
+                out=grouped[i][:].bitcast(F32).rearrange("p (b r u) -> p b r u", b=nb, u=2),
+                in_=turned[i][:].rearrange("p b u r -> p b r u"),
+            )
+
+        def quantize(i):
+            nc.vector.quantize_mx(out=x_codes[i][:].bitcast(E5M2X4), scales=x_scales[i][:], in_=grouped[i][:])
+
+        def spread_bias(h):
+            ps = accs.tile([P, HALF], BF16, tag="acc", name="bias_ps%d" % h)
+            nc.tensor.matmul(ps[:], lhsT=ones[:], rhs=bias_row[:, h * HALF : (h + 1) * HALF], start=True, stop=True)
+            bias_ps[h] = ps
+
+        def keep_bias(h):
+            nc.vector.tensor_copy(out=bias_all[h][:], in_=bias_ps[h][:])
+
+        def multiply(b, h):
+            i, j = where[b]
+            acc = accs.tile([P, HALF], F32, tag="acc", name="acc%d_%d" % (b, h))
+            nc.tensor.matmul_mx(
+                out=acc[:],
+                lhsT=x_codes[i][:, j * N : (j + 1) * N].bitcast(E5M2X4),
+                lhsT_scale=x_scales[i][:, j * N : (j + 1) * N],
+                rhs=w_codes[:, 2 * h * HALF : 2 * (h + 1) * HALF].bitcast(E2M1X4),
+                rhs_scale=w_scales[:, h * HALF : (h + 1) * HALF],
+                start=True,
+                stop=True,
+            )
+            sums[(b, h)] = acc
+
+        def add_bias(b, h):
+            cols = slice(h * HALF, (h + 1) * HALF)
+            nc.vector.tensor_tensor(out=q_sb[b][:, cols], in0=sums[(b, h)][:], in1=bias_all[h][:], op=ALU.add)
+
+        def store(b, cols):
+            nc.sync.dma_start(out=out_0[b][:, cols], in_=q_sb[b][:, cols])
+
+        def squares(b, cols, slot):
+            junk = rot.tile([P, D], F32, tag="junk", name="junk%d" % slot)
+            nc.scalar.activation(out=junk[:, cols], in_=q_sb[b][:, cols], func=ACT.Square, accum_out=sumsq[:, slot : slot + 1])
+
+        def root(b, src):
+            nc.gpsimd.tensor_tensor(out=norms[:, b : b + 1], in0=src, in1=half[:], op=ALU.pow)
+
+        whole = slice(0, D)
+        lo = slice(0, HALF)
+        hi = slice(HALF, D)
+
+        turn(0)
+        interleave(0)
+        spread_bias(0)
+        spread_bias(1)
+        quantize(0)
+        keep_bias(0)
+        keep_bias(1)
+        turn(1)
+        interleave(1)
+        quantize(1)
+        last = B - 1
+        for b in range(B):
+            multiply(b, 0)
+            multiply(b, 1)
+            if b > 0:
+                squares(b - 1, whole, b - 1)
+                root(b - 1, sumsq[:, b - 1 : b])
+            if b < 3:
+                turn(b + 2)
+                interleave(b + 2)
+            add_bias(b, 0)
+            if 1 <= b <= 3:
+                quantize(b + 1)
+            if b in (0, last):
+                store(b, lo)
+            add_bias(b, 1)
+            store(b, hi if b in (0, last) else whole)
+        split = 384
+        squares(last, slice(0, split), last)
+        junk_v = keep.tile([P, D - split], F32, name="junk_v")
+        sum_v = keep.tile([P, 1], F32, name="sum_v")
+        nc.vector.scalar_tensor_tensor(
+            out=junk_v[:], in0=q_sb[last][:, split:D], scalar=1.0, in1=q_sb[last][:, split:D],
+            op0=ALU.mult, op1=ALU.mult, accum_out=sum_v[:],
+        )
+        nc.gpsimd.tensor_tensor(out=sum_last[:], in0=sumsq[:, last : last + 1], in1=sum_v[:], op=ALU.add)
+        root(last, sum_last[:])
+
+        rows = tps.tile([P, P], F32, tag="tp", name="rows")
+        nc.tensor.transpose(rows[:], norms[:], ident[:])
+        neg_max = keep.tile([P, 1], F32, name="neg_max")
+        total = keep.tile([P, 1], F32, name="total")
+        inv_total = keep.tile([P, 1], F32, name="inv_total")
+        expo = keep.tile([P, N], F32, name="expo")
+        probs = keep.tile([P, N], F32, name="probs")
+        nc.vector.tensor_reduce(out=neg_max[0:B, :], in_=rows[0:B, :], axis=AX.X, op=ALU.max, negate=True)
+        nc.scalar.activation(out=expo[0:B, :], in_=rows[0:B, :], func=ACT.Exp, bias=neg_max[0:B, :], accum_out=total[0:B, :])
+        nc.vector.reciprocal(out=inv_total[0:B, :], in_=total[0:B, :])
+        nc.vector.tensor_scalar(out=probs[0:B, :], in0=expo[0:B, :], scalar1=inv_total[0:B, :], scalar2=None, op0=ALU.mult)
+        nc.sync.dma_start(out=out_1, in_=probs[0:B, :])

@@ -19,6 +19,7 @@ AX = mybir.AxisListType
 
 P = 128
 HALF = 512
+LOADS = [(0, 1), (1, 2), (2, 4), (4, 8)]
 GROUPS = [(0,), (1,), (2, 3), (4, 5), (6, 7)]
 
 
@@ -34,27 +35,21 @@ def tile_candidateaware_clickednewsattention_pa_kernel(tc, cand_topics, Wq_words
         ident = keep.tile([P, P], F32, name="ident")
         norms = keep.tile([P, P], F32, name="norms")
         ones = keep.tile([P, P], BF16, name="ones")
-        half = keep.tile([P, 1], F32, name="half")
+        half = keep.tile([P, 3], F32, name="half")
         bias_row = keep.tile([P, D], BF16, name="bias_row")
         bias_all = [keep.tile([P, HALF], BF16, name="bias_all%d" % h) for h in range(2)]
         w_codes = keep.tile([P, 2 * D], U8, name="w_codes", align_bytes=64)
         w_scales = keep.tile([P, D], U8, name="w_scales", align_bytes=64)
-        x_first = keep.tile([P, 1, K], BF16, name="x_first")
-        x_mid = keep.tile([P, 3, K], BF16, name="x_mid")
-        x_last = keep.tile([P, 4, K], BF16, name="x_last")
-        sumsq = keep.tile([P, B + 1], F32, name="sumsq")
-        sum_last = keep.tile([P, 1], F32, name="sum_last")
+        x_sb = [keep.tile([P, stop - first, K], BF16, name="x%d" % first) for first, stop in LOADS]
+        sumsq = keep.tile([P, B], F32, name="sumsq")
         q_sb = [keep.tile([P, D], F32, name="q%d" % b) for b in range(B)]
         grouped = [keep.tile([P, len(g) * K], BF16, name="grouped%d" % i, align_bytes=64) for i, g in enumerate(GROUPS)]
         x_codes = [keep.tile([P, len(g) * N], U32, name="x_codes%d" % i, align_bytes=64) for i, g in enumerate(GROUPS)]
         x_scales = [keep.tile([P, len(g) * N], U8, name="x_scales%d" % i, align_bytes=64) for i, g in enumerate(GROUPS)]
 
         def x_rows(b):
-            if b == 0:
-                return x_first[:, 0, :]
-            if b < 4:
-                return x_mid[:, b - 1, :]
-            return x_last[:, b - 4, :]
+            i = [first <= b < stop for first, stop in LOADS].index(True)
+            return x_sb[i][:, b - LOADS[i][0], :]
 
         where = {}
         for i, g in enumerate(GROUPS):
@@ -67,18 +62,23 @@ def tile_candidateaware_clickednewsattention_pa_kernel(tc, cand_topics, Wq_words
         make_identity(nc, ident[:])
         nc.gpsimd.memset(norms[:], 0.0)
 
-        nc.sync.dma_start(out=x_first[:, 0, :], in_=cand_topics[0])
-        nc.scalar.dma_start(out=bias_row[0:1, :], in_=bq.rearrange("(o n) -> o n", o=1))
+        def load_x(i):
+            first, stop = LOADS[i]
+            nc.sync.dma_start(out=x_sb[i][:], in_=cand_topics[first:stop].rearrange("b n k -> n b k"))
+
+        load_x(0)
         for quad in range(4):
             nc.sync.dma_start(
                 out=w_scales[32 * quad : 32 * quad + 4, :].bitcast(I32),
                 in_=Wq_scales[0, 4 * quad : 4 * quad + 4, :].bitcast(I32),
             )
-        nc.sync.dma_start(out=x_mid[:], in_=cand_topics[1:4].rearrange("b n k -> n b k"))
+        nc.sync.dma_start(out=bias_row[0:1, :], in_=bq.rearrange("(o n) -> o n", o=1))
+        load_x(1)
         nc.sync.dma_start(out=w_codes[:].bitcast(I32), in_=Wq_words[0].bitcast(I32))
-        nc.sync.dma_start(out=x_last[:], in_=cand_topics[4:8].rearrange("b n k -> n b k"))
+        for i in range(2, len(LOADS)):
+            load_x(i)
 
-        nc.scalar.activation(out=half[:], in_=ones[:, 0:1], func=ACT.Copy, scale=0.5)
+        nc.scalar.activation(out=half[:], in_=ones[:, 0:3], func=ACT.Copy, scale=0.5)
 
         turned = {}
         sums = {}
@@ -132,17 +132,19 @@ def tile_candidateaware_clickednewsattention_pa_kernel(tc, cand_topics, Wq_words
         def store(b, cols):
             nc.sync.dma_start(out=out_0[b][:, cols], in_=q_sb[b][:, cols])
 
-        def squares(b, cols, slot):
-            junk = rot.tile([P, D], F32, tag="junk", name="junk%d" % slot)
-            nc.scalar.activation(out=junk[:, cols], in_=q_sb[b][:, cols], func=ACT.Square, accum_out=sumsq[:, slot : slot + 1])
+        def squares(b, cols, total):
+            junk = rot.tile([P, D], F32, tag="junk", name="junk%d" % b)
+            nc.scalar.activation(out=junk[:, cols], in_=q_sb[b][:, cols], func=ACT.Square, accum_out=total)
 
-        def root(b, src):
-            nc.gpsimd.tensor_tensor(out=norms[:, b : b + 1], in0=src, in1=half[:], op=ALU.pow)
+        def root(first, count):
+            cols = slice(first, first + count)
+            nc.gpsimd.tensor_tensor(out=norms[:, cols], in0=sumsq[:, cols], in1=half[:, 0:count], op=ALU.pow)
 
         whole = slice(0, D)
         lo = slice(0, HALF)
         hi = slice(HALF, D)
 
+        last = B - 1
         turn(0)
         interleave(0)
         spread_bias(0)
@@ -153,13 +155,15 @@ def tile_candidateaware_clickednewsattention_pa_kernel(tc, cand_topics, Wq_words
         turn(1)
         interleave(1)
         quantize(1)
-        last = B - 1
         for b in range(B):
             multiply(b, 0)
             multiply(b, 1)
             if b > 0:
-                squares(b - 1, whole, b - 1)
-                root(b - 1, sumsq[:, b - 1 : b])
+                squares(b - 1, whole, sumsq[:, b - 1 : b])
+            if b == 3:
+                root(0, 3)
+            if 3 < b < last:
+                root(b - 1, 1)
             if b < 3:
                 turn(b + 2)
                 interleave(b + 2)
@@ -170,16 +174,15 @@ def tile_candidateaware_clickednewsattention_pa_kernel(tc, cand_topics, Wq_words
                 store(b, lo)
             add_bias(b, 1)
             store(b, hi if b in (0, last) else whole)
-        split = 384
-        squares(last, slice(0, split), last)
-        junk_v = keep.tile([P, D - split], F32, name="junk_v")
-        sum_v = keep.tile([P, 1], F32, name="sum_v")
+        junk_v = keep.tile([P, HALF], F32, name="junk_v")
+        parts = keep.tile([P, 2], F32, name="parts")
+        squares(last, lo, parts[:, 0:1])
         nc.vector.scalar_tensor_tensor(
-            out=junk_v[:], in0=q_sb[last][:, split:D], scalar=1.0, in1=q_sb[last][:, split:D],
-            op0=ALU.mult, op1=ALU.mult, accum_out=sum_v[:],
+            out=junk_v[:], in0=q_sb[last][:, hi], scalar=1.0, in1=q_sb[last][:, hi],
+            op0=ALU.mult, op1=ALU.mult, accum_out=parts[:, 1:2],
         )
-        nc.gpsimd.tensor_tensor(out=sum_last[:], in0=sumsq[:, last : last + 1], in1=sum_v[:], op=ALU.add)
-        root(last, sum_last[:])
+        nc.vector.tensor_tensor(out=sumsq[:, last : last + 1], in0=parts[:, 0:1], in1=parts[:, 1:2], op=ALU.add)
+        root(last - 1, 2)
 
         rows = tps.tile([P, P], F32, tag="tp", name="rows")
         nc.tensor.transpose(rows[:], norms[:], ident[:])

@@ -20,7 +20,7 @@ AX = mybir.AxisListType
 P = 128
 HALF = 512
 LOADS = [(0, 1), (1, 2), (2, 4), (4, 8)]
-GROUPS = [(0,), (1,), (2, 3), (4, 5), (6, 7)]
+GROUPS = [(0,), (1,), (2,), (3,), (4, 5), (6, 7)]
 
 
 def tile_candidateaware_clickednewsattention_pa_kernel(tc, cand_topics, Wq_words, Wq_scales, bq, out_0, out_1):
@@ -56,9 +56,9 @@ def tile_candidateaware_clickednewsattention_pa_kernel(tc, cand_topics, Wq_words
             for j, b in enumerate(g):
                 where[b] = (i, j)
 
+        nc.vector.memset(ones[:], 1.0)
         nc.vector.memset(w_scales[:].bitcast(I32), 0)
         nc.vector.memset(bias_row[:].bitcast(I32), 0)
-        nc.vector.memset(ones[:], 1.0)
         make_identity(nc, ident[:])
         nc.gpsimd.memset(norms[:], 0.0)
 
@@ -145,6 +145,9 @@ def tile_candidateaware_clickednewsattention_pa_kernel(tc, cand_topics, Wq_words
         hi = slice(HALF, D)
 
         last = B - 1
+        warm = accs.tile([P, 4, P], F32, tag="acc", name="warm")
+        for rep in range(3):
+            nc.tensor.matmul(warm[:], lhsT=ones[:], rhs=ones[:].unsqueeze(1).to_broadcast([P, 4, P]), start=True, stop=True)
         turn(0)
         interleave(0)
         spread_bias(0)
@@ -164,15 +167,20 @@ def tile_candidateaware_clickednewsattention_pa_kernel(tc, cand_topics, Wq_words
                 root(0, 3)
             if 3 < b < last:
                 root(b - 1, 1)
+            if b == 0:
+                turn(2)
+                interleave(2)
             if b < 3:
-                turn(b + 2)
-                interleave(b + 2)
+                turn(b + 3)
+                interleave(b + 3)
             add_bias(b, 0)
             if 1 <= b <= 3:
-                quantize(b + 1)
+                quantize(b + 2)
             if b in (0, last):
                 store(b, lo)
             add_bias(b, 1)
+            if b == 0:
+                quantize(2)
             store(b, hi if b in (0, last) else whole)
         junk_v = keep.tile([P, HALF], F32, name="junk_v")
         parts = keep.tile([P, 2], F32, name="parts")

from contextlib import ExitStack

import concourse.mybir as mybir
from concourse.masks import make_identity

B, N, K, D = 8, 128, 512, 1024
FLOPS = 2 * B * N * K * D

F32 = mybir.dt.float32
BF16 = mybir.dt.bfloat16
I32 = mybir.dt.int32
U32 = mybir.dt.uint32
U8 = mybir.dt.uint8
E5M2X4 = mybir.dt.float8_e5m2_x4
E2M1X4 = mybir.dt.float4_e2m1fn_x4
ACT = mybir.ActivationFunctionType
ALU = mybir.AluOpType
AX = mybir.AxisListType

P = 128
HALF = 512
LOADS = [(0, 1), (1, 2), (2, 4), (4, 8)]
GROUPS = [(0,), (1,), (2,), (3,), (4, 5), (6, 7)]


def tile_candidateaware_clickednewsattention_pa_kernel(tc, cand_topics, Wq_words, Wq_scales, bq, out_0, out_1):
    nc = tc.nc
    with ExitStack() as ctx:
        keep = ctx.enter_context(tc.tile_pool(name="keep", bufs=1))
        rot = ctx.enter_context(tc.tile_pool(name="rot", bufs=2))
        tps = ctx.enter_context(tc.psum_pool(name="tps", bufs=2))
        accs = ctx.enter_context(tc.psum_pool(name="accs", bufs=6))
        ctx.enter_context(tc.manual_schedule())

        ident = keep.tile([P, P], F32, name="ident")
        norms = keep.tile([P, P], F32, name="norms")
        ones = keep.tile([P, P], BF16, name="ones")
        half = keep.tile([P, 3], F32, name="half")
        bias_row = keep.tile([P, D], BF16, name="bias_row")
        bias_all = [keep.tile([P, HALF], BF16, name="bias_all%d" % h) for h in range(2)]
        w_codes = keep.tile([P, 2 * D], U8, name="w_codes", align_bytes=64)
        w_scales = keep.tile([P, D], U8, name="w_scales", align_bytes=64)
        x_sb = [keep.tile([P, stop - first, K], BF16, name="x%d" % first) for first, stop in LOADS]
        sumsq = keep.tile([P, B], F32, name="sumsq")
        q_sb = [keep.tile([P, D], F32, name="q%d" % b) for b in range(B)]
        grouped = [keep.tile([P, len(g) * K], BF16, name="grouped%d" % i, align_bytes=64) for i, g in enumerate(GROUPS)]
        x_codes = [keep.tile([P, len(g) * N], U32, name="x_codes%d" % i, align_bytes=64) for i, g in enumerate(GROUPS)]
        x_scales = [keep.tile([P, len(g) * N], U8, name="x_scales%d" % i, align_bytes=64) for i, g in enumerate(GROUPS)]

        def x_rows(b):
            i = [first <= b < stop for first, stop in LOADS].index(True)
            return x_sb[i][:, b - LOADS[i][0], :]

        where = {}
        for i, g in enumerate(GROUPS):
            for j, b in enumerate(g):
                where[b] = (i, j)

        nc.vector.memset(ones[:], 1.0)
        nc.vector.memset(w_scales[:].bitcast(I32), 0)
        nc.vector.memset(bias_row[:].bitcast(I32), 0)
        make_identity(nc, ident[:])
        nc.gpsimd.memset(norms[:], 0.0)

        def load_x(i):
            first, stop = LOADS[i]
            nc.sync.dma_start(out=x_sb[i][:], in_=cand_topics[first:stop].rearrange("b n k -> n b k"))

        load_x(0)
        for quad in range(4):
            nc.sync.dma_start(
                out=w_scales[32 * quad : 32 * quad + 4, :].bitcast(I32),
                in_=Wq_scales[0, 4 * quad : 4 * quad + 4, :].bitcast(I32),
            )
        nc.sync.dma_start(out=bias_row[0:1, :], in_=bq.rearrange("(o n) -> o n", o=1))
        load_x(1)
        nc.sync.dma_start(out=w_codes[:].bitcast(I32), in_=Wq_words[0].bitcast(I32))
        for i in range(2, len(LOADS)):
            load_x(i)

        nc.scalar.activation(out=half[:], in_=ones[:, 0:3], func=ACT.Copy, scale=0.5)

        turned = {}
        sums = {}
        bias_ps = {}

        def turn(i):
            g = GROUPS[i]
            xt = tps.tile([P, len(g), 2, N], F32, tag="tp", name="xt%d" % i)
            for j, b in enumerate(g):
                words = x_rows(b).bitcast(F32)
                for u in range(2):
                    nc.tensor.transpose(xt[:, j, u, :], words[:, u : K // 2 : 2], ident[:])
            turned[i] = xt

        def interleave(i):
            nb = len(GROUPS[i])
            nc.scalar.copy(
                out=grouped[i][:].bitcast(F32).rearrange("p (b r u) -> p b r u", b=nb, u=2),
                in_=turned[i][:].rearrange("p b u r -> p b r u"),
            )

        def quantize(i):
            nc.vector.quantize_mx(out=x_codes[i][:].bitcast(E5M2X4), scales=x_scales[i][:], in_=grouped[i][:])

        def spread_bias(h):
            ps = accs.tile([P, HALF], BF16, tag="acc", name="bias_ps%d" % h)
            nc.tensor.matmul(ps[:], lhsT=ones[:], rhs=bias_row[:, h * HALF : (h + 1) * HALF], start=True, stop=True)
            bias_ps[h] = ps

        def keep_bias(h):
            nc.vector.tensor_copy(out=bias_all[h][:], in_=bias_ps[h][:])

        def multiply(b, h):
            i, j = where[b]
            acc = accs.tile([P, HALF], F32, tag="acc", name="acc%d_%d" % (b, h))
            nc.tensor.matmul_mx(
                out=acc[:],
                lhsT=x_codes[i][:, j * N : (j + 1) * N].bitcast(E5M2X4),
                lhsT_scale=x_scales[i][:, j * N : (j + 1) * N],
                rhs=w_codes[:, 2 * h * HALF : 2 * (h + 1) * HALF].bitcast(E2M1X4),
                rhs_scale=w_scales[:, h * HALF : (h + 1) * HALF],
                start=True,
                stop=True,
            )
            sums[(b, h)] = acc

        def add_bias(b, h):
            cols = slice(h * HALF, (h + 1) * HALF)
            nc.vector.tensor_tensor(out=q_sb[b][:, cols], in0=sums[(b, h)][:], in1=bias_all[h][:], op=ALU.add)

        def store(b, cols):
            nc.sync.dma_start(out=out_0[b][:, cols], in_=q_sb[b][:, cols])

        def squares(b, cols, total):
            junk = rot.tile([P, D], F32, tag="junk", name="junk%d" % b)
            nc.scalar.activation(out=junk[:, cols], in_=q_sb[b][:, cols], func=ACT.Square, accum_out=total)

        def root(first, count):
            cols = slice(first, first + count)
            nc.gpsimd.tensor_tensor(out=norms[:, cols], in0=sumsq[:, cols], in1=half[:, 0:count], op=ALU.pow)

        whole = slice(0, D)
        lo = slice(0, HALF)
        hi = slice(HALF, D)

        last = B - 1
        warm = accs.tile([P, 4, P], F32, tag="acc", name="warm")
        for rep in range(3):
            nc.tensor.matmul(warm[:], lhsT=ones[:], rhs=ones[:].unsqueeze(1).to_broadcast([P, 4, P]), start=True, stop=True)
        turn(0)
        interleave(0)
        spread_bias(0)
        spread_bias(1)
        quantize(0)
        keep_bias(0)
        keep_bias(1)
        turn(1)
        interleave(1)
        quantize(1)
        for b in range(B):
            multiply(b, 0)
            multiply(b, 1)
            if b > 0:
                squares(b - 1, whole, sumsq[:, b - 1 : b])
            if b == 3:
                root(0, 3)
            if 3 < b < last:
                root(b - 1, 1)
            if b == 0:
                turn(2)
                interleave(2)
            if b < 3:
                turn(b + 3)
                interleave(b + 3)
            add_bias(b, 0)
            if 1 <= b <= 3:
                quantize(b + 2)
            if b in (0, last):
                store(b, lo)
            add_bias(b, 1)
            if b == 0:
                quantize(2)
            store(b, hi if b in (0, last) else whole)
        junk_v = keep.tile([P, HALF], F32, name="junk_v")
        parts = keep.tile([P, 2], F32, name="parts")
        squares(last, lo, parts[:, 0:1])
        nc.vector.scalar_tensor_tensor(
            out=junk_v[:], in0=q_sb[last][:, hi], scalar=1.0, in1=q_sb[last][:, hi],
            op0=ALU.mult, op1=ALU.mult, accum_out=parts[:, 1:2],
        )
        nc.vector.tensor_tensor(out=sumsq[:, last : last + 1], in0=parts[:, 0:1], in1=parts[:, 1:2], op=ALU.add)
        root(last - 1, 2)

        rows = tps.tile([P, P], F32, tag="tp", name="rows")
        nc.tensor.transpose(rows[:], norms[:], ident[:])
        neg_max = keep.tile([P, 1], F32, name="neg_max")
        total = keep.tile([P, 1], F32, name="total")
        inv_total = keep.tile([P, 1], F32, name="inv_total")
        expo = keep.tile([P, N], F32, name="expo")
        probs = keep.tile([P, N], F32, name="probs")
        nc.vector.tensor_reduce(out=neg_max[0:B, :], in_=rows[0:B, :], axis=AX.X, op=ALU.max, negate=True)
        nc.scalar.activation(out=expo[0:B, :], in_=rows[0:B, :], func=ACT.Exp, bias=neg_max[0:B, :], accum_out=total[0:B, :])
        nc.vector.reciprocal(out=inv_total[0:B, :], in_=total[0:B, :])
        nc.vector.tensor_scalar(out=probs[0:B, :], in0=expo[0:B, :], scalar1=inv_total[0:B, :], scalar2=None, op0=ALU.mult)
        nc.sync.dma_start(out=out_1, in_=probs[0:B, :])
